import numpy as np
import ml_dtypes


def mxq(x, axis, fmt="e4m3"):
    dtype, down = {"e4m3": (ml_dtypes.float8_e4m3fn, 7), "e5m2": (ml_dtypes.float8_e5m2, 14)}[fmt]
    v = np.moveaxis(np.asarray(x, np.float32).astype(ml_dtypes.bfloat16).astype(np.float64), axis, -1)
    blocks = v.reshape(v.shape[:-1] + (-1, 32))
    amax = np.abs(blocks).max(-1, keepdims=True)
    byte = np.maximum(np.where(amax > 0, np.frexp(amax)[1] - 1 + 127, 0) - down, 1)
    scale = np.exp2(byte - 127.0)
    codes = (blocks / scale).astype(np.float32).astype(dtype).astype(np.float64)
    return np.moveaxis((codes * scale).reshape(v.shape), -1, axis)


WIDE = False


def mx_kscale(k):
    if not WIDE:
        return np.ones(k)
    levels = np.array([10, -10, 5, -5, 0])
    a = np.random.permutation(np.resize(levels, k // 512 * 4)).reshape(k // 512, 4)
    idx = np.arange(k)
    return np.exp2(a[idx // 512, idx % 128 // 32])


BF16 = ml_dtypes.bfloat16


def bf(x):
    return np.asarray(x, np.float32).astype(BF16)


def f64(x):
    return np.asarray(x).astype(np.float64)


B, T, DIM, H, D = 4, 1024, 512, 4, 128
E = H * D


def softmax(z):
    e = np.exp(z - z.max(-1, keepdims=True))
    return e / e.sum(-1, keepdims=True)


def setup_inputs():
    u = mx_kscale(E).reshape(H, D)
    q = softmax(3.0 * np.random.standard_normal((B, H, T, D)))
    k_sum = (T / D) * np.exp(0.3 * np.random.standard_normal((B, H, 1, D)))
    amp = 2.0 * np.sqrt(T * np.mean(q * q))
    context = k_sum.transpose(0, 1, 3, 2) * 0.2 * np.random.standard_normal((1, H, 1, D)) + amp * np.random.standard_normal((B, H, D, D))
    return {"q": bf(q * u[None, :, None, :]),
            "k_sum": bf(k_sum / u[None, :, None, :]),
            "context": bf(context * u[None, :, None, :] / u[None, :, :, None]),
            "Wp": bf(np.random.standard_normal((DIM, E)) * 2.0 / np.sqrt(E) / u.reshape(E)),
            "bp": bf(np.random.standard_normal(DIM) * 0.2)}


def reference(q, k_sum, context, Wp, bp):
    d_inv = 1.0 / (f64(q) * f64(k_sum)).sum(axis=-1, keepdims=True)
    o = (f64(q) @ f64(context)) * d_inv + f64(q)
    o = o.transpose(0, 2, 1, 3).reshape(B, T, E)
    return (mxq(o, 2, "e4m3") @ mxq(f64(Wp), 1, "e4m3").T) + f64(bp)

@@ -1,0 +1,213 @@
+from contextlib import ExitStack
+
+import concourse.mybir as mybir
+from concourse.masks import make_identity
+
+BF16 = mybir.dt.bfloat16
+F32 = mybir.dt.float32
+U32 = mybir.dt.uint32
+U8 = mybir.dt.uint8
+FP8X4 = mybir.dt.float8_e4m3fn_x4
+MULT = mybir.AluOpType.mult
+ADD = mybir.AluOpType.add
+
+P = 128
+B, H, T, D = 4, 4, 1024, 128
+E = H * D
+DIM = 512
+SLOTS = T // P
+HALF = SLOTS // 2
+G = 2
+UNITS = G * H
+ROUNDS_PER_BATCH = SLOTS // G
+ROUNDS = B * ROUNDS_PER_BATCH
+
+FLOPS = 2 * B * H * T * D * D + 2 * B * H * T * D + 2 * B * T * E * DIM
+
+
+def tile_linearattention_pb_kernel(tc, q, k_sum, context, Wp, bp, out):
+    nc = tc.nc
+    with ExitStack() as stack:
+        const = stack.enter_context(tc.tile_pool(name="const", bufs=1))
+        work = stack.enter_context(tc.tile_pool(name="work", bufs=2))
+        results = stack.enter_context(tc.tile_pool(name="results", bufs=4))
+        psum = stack.enter_context(tc.psum_pool(name="psum", bufs=1))
+        stack.enter_context(tc.manual_schedule())
+
+        ident = const.tile([P, P], BF16)
+        make_identity(nc, ident[:])
+
+        ksum_rows = const.tile([P, D], BF16)
+        nc.vector.memset(ksum_rows[:], 0.0)
+        nc.sync.dma_start(out=ksum_rows[0 : B * H, :], in_=k_sum.rearrange("b h o d -> (b h o) d"))
+
+        bias = const.tile([P, DIM], BF16)
+        nc.scalar.dma_start(out=bias[:], in_=bp.partition_broadcast(P))
+
+        q_nat = {}
+        ctx = const.tile([P, B * H, D], BF16)
+        w_nat = const.tile([P, DIM // P, E], BF16)
+        for b in range(B):
+            q_view = q[b].rearrange("h (p j) d -> p h j d", j=SLOTS)
+            for half in range(SLOTS // HALF):
+                q_nat[(b, half)] = const.tile([P, H, HALF, D], BF16, name="q_nat_%d_%d" % (b, half))
+                nc.sync.dma_start(
+                    out=q_nat[(b, half)][:], in_=q_view[:, :, half * HALF : (half + 1) * HALF, :]
+                )
+                if half == 0:
+                    nc.sync.dma_start(
+                        out=ctx[:, b * H : (b + 1) * H, :], in_=context[b].rearrange("h d e -> d h e")
+                    )
+                if b == 0 and half == 0:
+                    nc.sync.dma_start(out=w_nat[:], in_=Wp.rearrange("(c p) k -> p c k", p=P))
+
+        ksum_bank = psum.tile([P, UNITS, P], BF16, tag="q_bank", bufs=2)
+        nc.tensor.transpose(ksum_bank[:, 0, :], ksum_rows[:], ident[:])
+        ksum_cols = const.tile([P, B * H], BF16)
+        nc.vector.tensor_copy(out=ksum_cols[:], in_=ksum_bank[:, 0, 0 : B * H])
+
+        w_codes = const.tile([P, DIM], U32, align_bytes=64)
+        w_scales = const.tile([P, DIM], U8, align_bytes=64)
+
+        def quantise_weights():
+            w_grouped = const.tile([P, DIM, H], BF16, align_bytes=64)
+            blocks_per_bank = UNITS // H
+            for first in range(0, DIM // P, blocks_per_bank):
+                w_bank = psum.tile([P, blocks_per_bank, H, P], BF16, tag="o_bank")
+                for c in range(blocks_per_bank):
+                    for h in range(H):
+                        nc.tensor.transpose(
+                            w_bank[:, c, h, :], w_nat[:, first + c, h * D : (h + 1) * D], ident[:]
+                        )
+                nc.scalar.copy(
+                    out=w_grouped[:, first * P : (first + blocks_per_bank) * P, :].rearrange(
+                        "p (c n) h -> p c n h", c=blocks_per_bank
+                    ),
+                    in_=w_bank[:].rearrange("p c h n -> p c n h"),
+                )
+            nc.vector.quantize_mx(
+                out=w_codes[:].bitcast(FP8X4),
+                scales=w_scales[:],
+                in_=w_grouped[:].rearrange("p n h -> p (n h)"),
+            )
+
+        live = {}
+
+        def queries(r, g, h):
+            b, pair = divmod(r, ROUNDS_PER_BATCH)
+            half, j = divmod(pair * G + g, HALF)
+            return q_nat[(b, half)][:, h, j, :]
+
+        def transpose_queries(r):
+            q_bank = psum.tile([P, UNITS, P], BF16, tag="q_bank", bufs=2)
+            for g in range(G):
+                for h in range(H):
+                    nc.tensor.transpose(q_bank[:, g * H + h, :], queries(r, g, h), ident[:])
+            q_t = work.tile([P, UNITS, P], BF16)
+            nc.scalar.copy(out=q_t[:], in_=q_bank[:])
+            live[("q_t", r)] = q_t
+
+        def multiply_context(r):
+            b = r // ROUNDS_PER_BATCH
+            q_t = live[("q_t", r)]
+            den_bank = psum.tile([P, UNITS], F32)
+            live[("den", r)] = den_bank
+            for g in range(G):
+                attn_bank = psum.tile([P, H, D], F32, tag="attn_bank_%d" % g, name="attn_bank")
+                live[("attn", r, g)] = attn_bank
+                for h in range(H):
+                    u = g * H + h
+                    nc.tensor.matmul(
+                        attn_bank[:, h, :], lhsT=q_t[:, u, :], rhs=ctx[:, b * H + h, :], start=True, stop=True
+                    )
+                    nc.tensor.matmul(
+                        den_bank[:, u : u + 1],
+                        lhsT=q_t[:, u, :],
+                        rhs=ksum_cols[:, b * H + h : b * H + h + 1],
+                        start=True,
+                        stop=True,
+                    )
+
+        def normalise(r):
+            d_inv = work.tile([P, UNITS], F32)
+            nc.vector.reciprocal(out=d_inv[:], in_=live[("den", r)][:])
+            om = work.tile([P, G, E], BF16)
+            for g in range(G):
+                for h in range(H):
+                    u = g * H + h
+                    nc.vector.scalar_tensor_tensor(
+                        out=om[:, g, h * D : (h + 1) * D],
+                        in0=live[("attn", r, g)][:, h, :],
+                        scalar=d_inv[:, u : u + 1],
+                        in1=queries(r, g, h),
+                        op0=MULT,
+                        op1=ADD,
+                    )
+            live[("om", r)] = om
+
+        def transpose_outputs(r):
+            om = live[("om", r)]
+            o_bank = psum.tile([P, G, H, P], BF16, tag="o_bank")
+            for g in range(G):
+                for h in range(H):
+                    nc.tensor.transpose(o_bank[:, g, h, :], om[:, g, h * D : (h + 1) * D], ident[:])
+            grouped = work.tile([P, G, P, H], BF16, align_bytes=64)
+            nc.scalar.copy(out=grouped[:], in_=o_bank[:].rearrange("p g h t -> p g t h"))
+            live[("grouped", r)] = grouped
+
+        def quantise(r):
+            codes = work.tile([P, G * P], U32, align_bytes=64)
+            scales = work.tile([P, G * P], U8, align_bytes=64)
+            nc.vector.quantize_mx(
+                out=codes[:].bitcast(FP8X4),
+                scales=scales[:],
+                in_=live[("grouped", r)][:].rearrange("p g t h -> p (g t h)"),
+            )
+            live[("codes", r)] = codes
+            live[("scales", r)] = scales
+
+        def project(r):
+            for g in range(G):
+                tokens = slice(g * P, (g + 1) * P)
+                out_bank = psum.tile([P, DIM], F32, tag="out_bank_%d" % g, name="out_bank")
+                nc.tensor.matmul_mx(
+                    out=out_bank[:],
+                    lhsT=live[("codes", r)][:, tokens].bitcast(FP8X4),
+                    lhsT_scale=live[("scales", r)][:, tokens],
+                    rhs=w_codes[:].bitcast(FP8X4),
+                    rhs_scale=w_scales[:],
+                    start=True,
+                    stop=True,
+                )
+                live[("out", r, g)] = out_bank
+
+        def add_bias_and_store(r):
+            b, pair = divmod(r, ROUNDS_PER_BATCH)
+            result = results.tile([P, G, DIM], F32)
+            for g in range(G):
+                nc.vector.tensor_tensor(out=result[:, g, :], in0=live[("out", r, g)][:], in1=bias[:], op=ADD)
+            out_view = out[b].rearrange("(p j) n -> p j n", j=SLOTS)
+            nc.sync.dma_start(out=out_view[:, pair * G : (pair + 1) * G, :], in_=result[:])
+
+        def active(r):
+            return 0 <= r < ROUNDS
+
+        transpose_queries(0)
+        multiply_context(0)
+        normalise(0)
+        quantise_weights()
+        for s in range(ROUNDS + 2):
+            if active(s + 1):
+                transpose_queries(s + 1)
+            if active(s):
+                transpose_outputs(s)
+            if active(s + 1):
+                multiply_context(s + 1)
+            if active(s - 1):
+                quantise(s - 1)
+            if active(s - 2):
+                add_bias_and_store(s - 2)
+            if active(s - 1):
+                project(s - 1)
+            if active(s + 1):
+                normalise(s + 1)

@@ -32,7 +32,6 @@ def tile_linearattention_pb_kernel(tc, q, k_sum, context, Wp, bp, out):
         work = stack.enter_context(tc.tile_pool(name="work", bufs=2))
         results = stack.enter_context(tc.tile_pool(name="results", bufs=4))
         psum = stack.enter_context(tc.psum_pool(name="psum", bufs=1))
-        stack.enter_context(tc.manual_schedule())
 
         ident = const.tile([P, P], BF16)
         make_identity(nc, ident[:])
@@ -189,25 +188,13 @@ def tile_linearattention_pb_kernel(tc, q, k_sum, context, Wp, bp, out):
             out_view = out[b].rearrange("(p j) n -> p j n", j=SLOTS)
             nc.sync.dma_start(out=out_view[:, pair * G : (pair + 1) * G, :], in_=result[:])
 
-        def active(r):
-            return 0 <= r < ROUNDS
-
-        transpose_queries(0)
-        multiply_context(0)
-        normalise(0)
-        quantise_weights()
-        for s in range(ROUNDS + 2):
-            if active(s + 1):
-                transpose_queries(s + 1)
-            if active(s):
-                transpose_outputs(s)
-            if active(s + 1):
-                multiply_context(s + 1)
-            if active(s - 1):
-                quantise(s - 1)
-            if active(s - 2):
-                add_bias_and_store(s - 2)
-            if active(s - 1):
-                project(s - 1)
-            if active(s + 1):
-                normalise(s + 1)
+        for r in range(ROUNDS):
+            transpose_queries(r)
+            multiply_context(r)
+            normalise(r)
+            if r == 0:
+                quantise_weights()
+            transpose_outputs(r)
+            quantise(r)
+            project(r)
+            add_bias_and_store(r)

@@ -40,8 +40,10 @@ def tile_linearattention_pb_kernel(tc, q, k_sum, context, Wp, bp, out):
         nc.vector.memset(ksum_rows[:], 0.0)
         nc.sync.dma_start(out=ksum_rows[0 : B * H, :], in_=k_sum.rearrange("b h o d -> (b h o) d"))
 
-        bias = const.tile([P, DIM], BF16)
-        nc.scalar.dma_start(out=bias[:], in_=bp.partition_broadcast(P))
+        bias_bf16 = const.tile([P, DIM], BF16)
+        nc.scalar.dma_start(out=bias_bf16[:], in_=bp.partition_broadcast(P))
+        bias = const.tile([P, DIM], F32)
+        nc.vector.tensor_copy(out=bias[:], in_=bias_bf16[:])
 
         q_nat = {}
         ctx = const.tile([P, B * H, D], BF16)
@@ -183,8 +185,9 @@ def tile_linearattention_pb_kernel(tc, q, k_sum, context, Wp, bp, out):
         def add_bias_and_store(r):
             b, pair = divmod(r, ROUNDS_PER_BATCH)
             result = results.tile([P, G, DIM], F32)
-            for g in range(G):
-                nc.vector.tensor_tensor(out=result[:, g, :], in0=live[("out", r, g)][:], in1=bias[:], op=ADD)
+            nc.vector.tensor_tensor(out=result[:, 0, :], in0=live[("out", r, 0)][:], in1=bias[:], op=ADD)
+            nc.scalar.copy(out=result[:, 1, :], in_=live[("out", r, 1)][:])
+            nc.gpsimd.tensor_tensor(out=result[:, 1, :], in0=result[:, 1, :], in1=bias[:], op=ADD)
             out_view = out[b].rearrange("(p j) n -> p j n", j=SLOTS)
             nc.sync.dma_start(out=out_view[:, pair * G : (pair + 1) * G, :], in_=result[:])
 

@@ -32,6 +32,7 @@ def tile_linearattention_pb_kernel(tc, q, k_sum, context, Wp, bp, out):
         work = stack.enter_context(tc.tile_pool(name="work", bufs=2))
         results = stack.enter_context(tc.tile_pool(name="results", bufs=4))
         psum = stack.enter_context(tc.psum_pool(name="psum", bufs=1))
+        stack.enter_context(tc.manual_schedule())
 
         ident = const.tile([P, P], BF16)
         make_identity(nc, ident[:])
@@ -40,10 +41,8 @@ def tile_linearattention_pb_kernel(tc, q, k_sum, context, Wp, bp, out):
         nc.vector.memset(ksum_rows[:], 0.0)
         nc.sync.dma_start(out=ksum_rows[0 : B * H, :], in_=k_sum.rearrange("b h o d -> (b h o) d"))
 
-        bias_bf16 = const.tile([P, DIM], BF16)
-        nc.scalar.dma_start(out=bias_bf16[:], in_=bp.partition_broadcast(P))
-        bias = const.tile([P, DIM], F32)
-        nc.vector.tensor_copy(out=bias[:], in_=bias_bf16[:])
+        bias = const.tile([P, DIM], BF16)
+        nc.scalar.dma_start(out=bias[:], in_=bp.partition_broadcast(P))
 
         q_nat = {}
         ctx = const.tile([P, B * H, D], BF16)
@@ -62,7 +61,7 @@ def tile_linearattention_pb_kernel(tc, q, k_sum, context, Wp, bp, out):
                 if b == 0 and half == 0:
                     nc.sync.dma_start(out=w_nat[:], in_=Wp.rearrange("(c p) k -> p c k", p=P))
 
-        ksum_bank = psum.tile([P, UNITS, P], BF16, tag="q_bank", bufs=2)
+        ksum_bank = psum.tile([P, UNITS, P], BF16, tag="q_bank")
         nc.tensor.transpose(ksum_bank[:, 0, :], ksum_rows[:], ident[:])
         ksum_cols = const.tile([P, B * H], BF16)
         nc.vector.tensor_copy(out=ksum_cols[:], in_=ksum_bank[:, 0, 0 : B * H])
@@ -73,14 +72,16 @@ def tile_linearattention_pb_kernel(tc, q, k_sum, context, Wp, bp, out):
         def quantise_weights():
             w_grouped = const.tile([P, DIM, H], BF16, align_bytes=64)
             blocks_per_bank = UNITS // H
-            for first in range(0, DIM // P, blocks_per_bank):
-                w_bank = psum.tile([P, blocks_per_bank, H, P], BF16, tag="o_bank")
+            copies = [nc.scalar.copy, nc.vector.tensor_copy]
+            for g in range(G):
+                first = g * blocks_per_bank
+                w_bank = psum.tile([P, blocks_per_bank, H, P], BF16, tag="out_bank_%d" % g, name="w_bank")
                 for c in range(blocks_per_bank):
                     for h in range(H):
                         nc.tensor.transpose(
                             w_bank[:, c, h, :], w_nat[:, first + c, h * D : (h + 1) * D], ident[:]
                         )
-                nc.scalar.copy(
+                copies[g](
                     out=w_grouped[:, first * P : (first + blocks_per_bank) * P, :].rearrange(
                         "p (c n) h -> p c n h", c=blocks_per_bank
                     ),
@@ -100,7 +101,7 @@ def tile_linearattention_pb_kernel(tc, q, k_sum, context, Wp, bp, out):
             return q_nat[(b, half)][:, h, j, :]
 
         def transpose_queries(r):
-            q_bank = psum.tile([P, UNITS, P], BF16, tag="q_bank", bufs=2)
+            q_bank = psum.tile([P, UNITS, P], BF16, tag="q_bank")
             for g in range(G):
                 for h in range(H):
                     nc.tensor.transpose(q_bank[:, g * H + h, :], queries(r, g, h), ident[:])
@@ -114,7 +115,7 @@ def tile_linearattention_pb_kernel(tc, q, k_sum, context, Wp, bp, out):
             den_bank = psum.tile([P, UNITS], F32)
             live[("den", r)] = den_bank
             for g in range(G):
-                attn_bank = psum.tile([P, H, D], F32, tag="attn_bank_%d" % g, name="attn_bank")
+                attn_bank = psum.tile([P, H, D], F32, bufs=3)
                 live[("attn", r, g)] = attn_bank
                 for h in range(H):
                     u = g * H + h
@@ -152,6 +153,10 @@ def tile_linearattention_pb_kernel(tc, q, k_sum, context, Wp, bp, out):
             for g in range(G):
                 for h in range(H):
                     nc.tensor.transpose(o_bank[:, g, h, :], om[:, g, h * D : (h + 1) * D], ident[:])
+            live[("o_bank", r)] = o_bank
+
+        def regroup_outputs(r):
+            o_bank = live[("o_bank", r)]
             grouped = work.tile([P, G, P, H], BF16, align_bytes=64)
             nc.scalar.copy(out=grouped[:], in_=o_bank[:].rearrange("p g h t -> p g t h"))
             live[("grouped", r)] = grouped
@@ -185,19 +190,30 @@ def tile_linearattention_pb_kernel(tc, q, k_sum, context, Wp, bp, out):
         def add_bias_and_store(r):
             b, pair = divmod(r, ROUNDS_PER_BATCH)
             result = results.tile([P, G, DIM], F32)
-            nc.vector.tensor_tensor(out=result[:, 0, :], in0=live[("out", r, 0)][:], in1=bias[:], op=ADD)
-            nc.scalar.copy(out=result[:, 1, :], in_=live[("out", r, 1)][:])
-            nc.gpsimd.tensor_tensor(out=result[:, 1, :], in0=result[:, 1, :], in1=bias[:], op=ADD)
+            for g in range(G):
+                nc.vector.tensor_tensor(out=result[:, g, :], in0=live[("out", r, g)][:], in1=bias[:], op=ADD)
             out_view = out[b].rearrange("(p j) n -> p j n", j=SLOTS)
             nc.sync.dma_start(out=out_view[:, pair * G : (pair + 1) * G, :], in_=result[:])
 
-        for r in range(ROUNDS):
-            transpose_queries(r)
-            multiply_context(r)
-            normalise(r)
-            if r == 0:
+        def active(r):
+            return 0 <= r < ROUNDS
+
+        for c in range(-2, ROUNDS + 2):
+            if active(c - 1):
+                regroup_outputs(c - 1)
+            if active(c - 2):
+                project(c - 2)
+            if active(c + 2):
+                transpose_queries(c + 2)
+            if active(c):
+                normalise(c)
+            if active(c + 1):
+                multiply_context(c + 1)
+            if active(c):
+                transpose_outputs(c)
+            if c == 0:
                 quantise_weights()
-            transpose_outputs(r)
-            quantise(r)
-            project(r)
-            add_bias_and_store(r)
+            if active(c - 2):
+                add_bias_and_store(c - 2)
+            if active(c - 1):
+                quantise(c - 1)

from contextlib import ExitStack

import concourse.mybir as mybir
from concourse.masks import make_identity

BF16 = mybir.dt.bfloat16
F32 = mybir.dt.float32
U32 = mybir.dt.uint32
U8 = mybir.dt.uint8
FP8X4 = mybir.dt.float8_e4m3fn_x4
MULT = mybir.AluOpType.mult
ADD = mybir.AluOpType.add

P = 128
B, H, T, D = 4, 4, 1024, 128
E = H * D
DIM = 512
SLOTS = T // P
HALF = SLOTS // 2
G = 2
UNITS = G * H
ROUNDS_PER_BATCH = SLOTS // G
ROUNDS = B * ROUNDS_PER_BATCH

FLOPS = 2 * B * H * T * D * D + 2 * B * H * T * D + 2 * B * T * E * DIM


def tile_linearattention_pb_kernel(tc, q, k_sum, context, Wp, bp, out):
    nc = tc.nc
    with ExitStack() as stack:
        const = stack.enter_context(tc.tile_pool(name="const", bufs=1))
        work = stack.enter_context(tc.tile_pool(name="work", bufs=2))
        results = stack.enter_context(tc.tile_pool(name="results", bufs=4))
        psum = stack.enter_context(tc.psum_pool(name="psum", bufs=1))
        stack.enter_context(tc.manual_schedule())

        ident = const.tile([P, P], BF16)
        make_identity(nc, ident[:])

        ksum_rows = const.tile([P, D], BF16)
        nc.vector.memset(ksum_rows[:], 0.0)
        nc.sync.dma_start(out=ksum_rows[0 : B * H, :], in_=k_sum.rearrange("b h o d -> (b h o) d"))

        bias = const.tile([P, DIM], BF16)
        nc.scalar.dma_start(out=bias[:], in_=bp.partition_broadcast(P))

        q_nat = {}
        ctx = const.tile([P, B * H, D], BF16)
        w_nat = const.tile([P, DIM // P, E], BF16)
        for b in range(B):
            q_view = q[b].rearrange("h (p j) d -> p h j d", j=SLOTS)
            for half in range(SLOTS // HALF):
                q_nat[(b, half)] = const.tile([P, H, HALF, D], BF16, name="q_nat_%d_%d" % (b, half))
                nc.sync.dma_start(
                    out=q_nat[(b, half)][:], in_=q_view[:, :, half * HALF : (half + 1) * HALF, :]
                )
                if half == 0:
                    nc.sync.dma_start(
                        out=ctx[:, b * H : (b + 1) * H, :], in_=context[b].rearrange("h d e -> d h e")
                    )
                if b == 0 and half == 0:
                    nc.sync.dma_start(out=w_nat[:], in_=Wp.rearrange("(c p) k -> p c k", p=P))

        ksum_bank = psum.tile([P, UNITS, P], BF16, tag="q_bank")
        nc.tensor.transpose(ksum_bank[:, 0, :], ksum_rows[:], ident[:])
        ksum_cols = const.tile([P, B * H], BF16)
        nc.vector.tensor_copy(out=ksum_cols[:], in_=ksum_bank[:, 0, 0 : B * H])

        w_codes = const.tile([P, DIM], U32, align_bytes=64)
        w_scales = const.tile([P, DIM], U8, align_bytes=64)

        def quantise_weights():
            w_grouped = const.tile([P, DIM, H], BF16, align_bytes=64)
            blocks_per_bank = UNITS // H
            copies = [nc.scalar.copy, nc.vector.tensor_copy]
            for g in range(G):
                first = g * blocks_per_bank
                w_bank = psum.tile([P, blocks_per_bank, H, P], BF16, tag="out_bank_%d" % g, name="w_bank")
                for c in range(blocks_per_bank):
                    for h in range(H):
                        nc.tensor.transpose(
                            w_bank[:, c, h, :], w_nat[:, first + c, h * D : (h + 1) * D], ident[:]
                        )
                copies[g](
                    out=w_grouped[:, first * P : (first + blocks_per_bank) * P, :].rearrange(
                        "p (c n) h -> p c n h", c=blocks_per_bank
                    ),
                    in_=w_bank[:].rearrange("p c h n -> p c n h"),
                )
            nc.vector.quantize_mx(
                out=w_codes[:].bitcast(FP8X4),
                scales=w_scales[:],
                in_=w_grouped[:].rearrange("p n h -> p (n h)"),
            )

        live = {}

        def queries(r, g, h):
            b, pair = divmod(r, ROUNDS_PER_BATCH)
            half, j = divmod(pair * G + g, HALF)
            return q_nat[(b, half)][:, h, j, :]

        def transpose_queries(r):
            q_bank = psum.tile([P, UNITS, P], BF16, tag="q_bank")
            for g in range(G):
                for h in range(H):
                    nc.tensor.transpose(q_bank[:, g * H + h, :], queries(r, g, h), ident[:])
            q_t = work.tile([P, UNITS, P], BF16)
            nc.scalar.copy(out=q_t[:], in_=q_bank[:])
            live[("q_t", r)] = q_t

        def multiply_context(r):
            b = r // ROUNDS_PER_BATCH
            q_t = live[("q_t", r)]
            den_bank = psum.tile([P, UNITS], F32)
            live[("den", r)] = den_bank
            for g in range(G):
                attn_bank = psum.tile([P, H, D], F32, bufs=3)
                live[("attn", r, g)] = attn_bank
                for h in range(H):
                    u = g * H + h
                    nc.tensor.matmul(
                        attn_bank[:, h, :], lhsT=q_t[:, u, :], rhs=ctx[:, b * H + h, :], start=True, stop=True
                    )
                    nc.tensor.matmul(
                        den_bank[:, u : u + 1],
                        lhsT=q_t[:, u, :],
                        rhs=ksum_cols[:, b * H + h : b * H + h + 1],
                        start=True,
                        stop=True,
                    )

        def normalise(r):
            d_inv = work.tile([P, UNITS], F32)
            nc.vector.reciprocal(out=d_inv[:], in_=live[("den", r)][:])
            om = work.tile([P, G, E], BF16)
            for g in range(G):
                for h in range(H):
                    u = g * H + h
                    nc.vector.scalar_tensor_tensor(
                        out=om[:, g, h * D : (h + 1) * D],
                        in0=live[("attn", r, g)][:, h, :],
                        scalar=d_inv[:, u : u + 1],
                        in1=queries(r, g, h),
                        op0=MULT,
                        op1=ADD,
                    )
            live[("om", r)] = om

        def transpose_outputs(r):
            om = live[("om", r)]
            o_bank = psum.tile([P, G, H, P], BF16, tag="o_bank")
            for g in range(G):
                for h in range(H):
                    nc.tensor.transpose(o_bank[:, g, h, :], om[:, g, h * D : (h + 1) * D], ident[:])
            live[("o_bank", r)] = o_bank

        def regroup_outputs(r):
            o_bank = live[("o_bank", r)]
            grouped = work.tile([P, G, P, H], BF16, align_bytes=64)
            nc.scalar.copy(out=grouped[:], in_=o_bank[:].rearrange("p g h t -> p g t h"))
            live[("grouped", r)] = grouped

        def quantise(r):
            codes = work.tile([P, G * P], U32, align_bytes=64)
            scales = work.tile([P, G * P], U8, align_bytes=64)
            nc.vector.quantize_mx(
                out=codes[:].bitcast(FP8X4),
                scales=scales[:],
                in_=live[("grouped", r)][:].rearrange("p g t h -> p (g t h)"),
            )
            live[("codes", r)] = codes
            live[("scales", r)] = scales

        def project(r):
            for g in range(G):
                tokens = slice(g * P, (g + 1) * P)
                out_bank = psum.tile([P, DIM], F32, tag="out_bank_%d" % g, name="out_bank")
                nc.tensor.matmul_mx(
                    out=out_bank[:],
                    lhsT=live[("codes", r)][:, tokens].bitcast(FP8X4),
                    lhsT_scale=live[("scales", r)][:, tokens],
                    rhs=w_codes[:].bitcast(FP8X4),
                    rhs_scale=w_scales[:],
                    start=True,
                    stop=True,
                )
                live[("out", r, g)] = out_bank

        def add_bias_and_store(r):
            b, pair = divmod(r, ROUNDS_PER_BATCH)
            result = results.tile([P, G, DIM], F32)
            for g in range(G):
                nc.vector.tensor_tensor(out=result[:, g, :], in0=live[("out", r, g)][:], in1=bias[:], op=ADD)
            out_view = out[b].rearrange("(p j) n -> p j n", j=SLOTS)
            nc.sync.dma_start(out=out_view[:, pair * G : (pair + 1) * G, :], in_=result[:])

        def active(r):
            return 0 <= r < ROUNDS

        for c in range(-2, ROUNDS + 2):
            if active(c - 1):
                regroup_outputs(c - 1)
            if active(c - 2):
                project(c - 2)
            if active(c + 2):
                transpose_queries(c + 2)
            if active(c):
                normalise(c)
            if active(c + 1):
                multiply_context(c + 1)
            if active(c):
                transpose_outputs(c)
            if c == 0:
                quantise_weights()
            if active(c - 2):
                add_bias_and_store(c - 2)
            if active(c - 1):
                quantise(c - 1)
